import numpy as np
import ml_dtypes


BF16 = ml_dtypes.bfloat16


def bf(x):
    return np.asarray(x, np.float32).astype(BF16)


def f64(x):
    return np.asarray(x).astype(np.float64)


E2M1 = np.array([0.0, 0.5, 1.0, 1.5, 2.0, 3.0, 4.0, 6.0, -0.0, -0.5, -1.0, -1.5, -2.0, -3.0, -4.0, -6.0])


def pack_weight(w, fmt):
    k, n = w.shape
    w = f64(bf(w)).reshape(k // 32, 32, n)
    amax = np.abs(w).max(1)
    if fmt == "e4m3":
        byte = np.frexp(amax)[1] - 1 + 127 - 7
    else:
        mant, ex = np.frexp(amax / 6.0)
        byte = np.where(mant > 0.5, ex, ex - 1) + 127
    byte = np.clip(np.where(amax > 0, byte, 1), 1, 254)
    scaled = (w * np.exp2(127.0 - byte)[:, None, :]).reshape(k, n).astype(np.float32)
    by_word = np.ascontiguousarray(scaled.reshape(k // 512, 128, 4, n).transpose(0, 1, 3, 2))
    if fmt == "e4m3":
        words = by_word.astype(ml_dtypes.float8_e4m3fn).view(np.uint8)
    else:
        c = by_word.astype(ml_dtypes.float4_e2m1fn).view(np.uint8) & 0xF
        words = c[..., 0::2] | (c[..., 1::2] << 4)
    return np.ascontiguousarray(words), np.ascontiguousarray(byte.astype(np.uint8).reshape(k // 512, 16, n))


def unpack_weight(words, scales, fmt):
    g, p, n, _ = words.shape
    if fmt == "e4m3":
        vals = np.ascontiguousarray(words).view(ml_dtypes.float8_e4m3fn).astype(np.float64)
    else:
        nib = np.empty((g, p, n, 4), np.uint8)
        nib[..., 0::2] = words & 0xF
        nib[..., 1::2] = words >> 4
        vals = E2M1[nib]
    vals = vals * np.repeat(np.exp2(scales.astype(np.float64) - 127.0), 8, axis=1)[..., None]
    return vals.transpose(0, 1, 3, 2).reshape(g * 512, n)

def pack4(w):
    words, scales = pack_weight(w, "e2m1")
    return words.reshape(words.shape[0], 128, -1), scales


def unpack4(words, scales):
    return unpack_weight(words.reshape(words.shape[0], 128, -1, 2), scales, "e2m1")


def kspread(k):
    return np.exp2(np.repeat(np.random.randint(-6, 7, k // 32), 32).astype(np.float64))


B, G, DB, DR = 128, 16, 1536, 3072


def mish(v):
    return v * np.tanh(np.log(1.0 + np.exp(v)))


def setup_inputs():
    s, t = kspread(DR), kspread(DB)
    BB_feature = np.random.standard_normal((B, G, DB)) * t
    RF_feature = np.random.standard_normal((B, DR)) * s
    W_bbbb = np.random.standard_normal((DB, DB)) / np.sqrt(DB) / t
    b_bbbb = bf(np.random.standard_normal(DB) * 0.5)
    W_rfbb = np.random.standard_normal((DB, DR)) / np.sqrt(DR) / s
    b_rfbb = bf(np.random.standard_normal(DB) * 0.5)
    BB_feature_words, BB_feature_scales = pack4(np.ascontiguousarray(BB_feature.reshape(B * G, DB).T))
    RF_feature_words, RF_feature_scales = pack4(np.ascontiguousarray(RF_feature.T))
    W_bbbb_words, W_bbbb_scales = pack4(np.ascontiguousarray(W_bbbb.T))
    W_rfbb_words, W_rfbb_scales = pack4(np.ascontiguousarray(W_rfbb.T))
    return {"BB_feature_words": BB_feature_words,
            "BB_feature_scales": BB_feature_scales,
            "RF_feature_words": RF_feature_words,
            "RF_feature_scales": RF_feature_scales,
            "W_bbbb_words": W_bbbb_words,
            "W_bbbb_scales": W_bbbb_scales,
            "b_bbbb": b_bbbb,
            "W_rfbb_words": W_rfbb_words,
            "W_rfbb_scales": W_rfbb_scales,
            "b_rfbb": b_rfbb}


def reference(BB_feature_words, BB_feature_scales, RF_feature_words, RF_feature_scales, W_bbbb_words, W_bbbb_scales, b_bbbb, W_rfbb_words, W_rfbb_scales, b_rfbb):
    RF_to_BB = mish((unpack4(RF_feature_words, RF_feature_scales).T @ unpack4(W_rfbb_words, W_rfbb_scales)) + f64(b_rfbb))
    BB_to_BB = mish((unpack4(BB_feature_words, BB_feature_scales).T.reshape(B, G, DB) @ unpack4(W_bbbb_words, W_bbbb_scales)) + f64(b_bbbb))
    return BB_to_BB + RF_to_BB[:, None, :]

@@ -1,0 +1,292 @@
+from contextlib import ExitStack
+
+import concourse.mybir as mybir
+from concourse.masks import make_identity
+
+F32 = mybir.dt.float32
+BF16 = mybir.dt.bfloat16
+U8 = mybir.dt.uint8
+I32 = mybir.dt.int32
+FP4 = mybir.dt.float4_e2m1fn_x4
+ACT = mybir.ActivationFunctionType
+ALU = mybir.AluOpType
+
+P = 128
+B, G, DB, DR = 128, 16, 1536, 3072
+GB, GR = DB // 512, DR // 512
+NB = DB // P
+TOK = B * G
+NT = TOK // 512
+BQ = 512 // G
+FLOPS = 2 * TOK * DB * DB + 2 * B * DR * DB
+TINY = 1e-18
+
+GPS_MULT = {2, 4, 5}
+
+
+def tile_gnn_layer_pb_kernel(tc, bb_words, bb_scales, rf_words, rf_scales, w_words, w_scales, b_bb, wr_words, wr_scales, b_rf, out):
+    nc = tc.nc
+    with ExitStack() as ctx:
+        keep = ctx.enter_context(tc.tile_pool(name="keep", bufs=1))
+        ypool = ctx.enter_context(tc.tile_pool(name="ypool", bufs=9))
+        tpool = ctx.enter_context(tc.tile_pool(name="tpool", bufs=9))
+        opool = ctx.enter_context(tc.tile_pool(name="opool", bufs=2))
+        pmx = ctx.enter_context(tc.psum_pool(name="pmx", bufs=4))
+        ptr = ctx.enter_context(tc.psum_pool(name="ptr", bufs=4))
+        ctx.enter_context(tc.manual_schedule())
+
+        dummy = keep.tile([P, 1], F32, name="dummy")
+        w_pl = keep.tile([P, GB, DB], U8, name="w_pl", align_bytes=64)
+        bb_pl = keep.tile([P, GB, TOK], U8, name="bb_pl", align_bytes=64)
+        rf_pl = keep.tile([P, GR, B], U8, name="rf_pl", align_bytes=64)
+        wr_pl = keep.tile([P, GR, DB], U8, name="wr_pl", align_bytes=64)
+        bias_rows = keep.tile([P, P], BF16, name="bias_rows")
+        bias = keep.tile([P, 2 * NB], F32, name="bias")
+        negb = keep.tile([P, 2], F32, name="negb")
+        tiny = keep.tile([P, 1], F32, name="tiny")
+        half = keep.tile([P, 1], F32, name="half")
+        ident_b = keep.tile([P, P], BF16, name="ident_b")
+        ident = keep.tile([P, P], F32, name="ident")
+        r_tok = keep.tile([P, DB], F32, name="r_tok")
+
+        nc.vector.memset(w_pl[:].bitcast(I32), 0)
+        nc.vector.memset(bb_pl[:].bitcast(I32), 0)
+        nc.gpsimd.memset(dummy[:], 0.0)
+        nc.gpsimd.memset(bias_rows[:], 0.0)
+        nc.gpsimd.memset(tiny[:], TINY)
+        nc.gpsimd.memset(half[:], 0.5)
+        make_identity(nc, ident_b[:])
+        make_identity(nc, ident[:])
+        nc.vector.memset(rf_pl[:].bitcast(I32), 0)
+        nc.vector.memset(wr_pl[:].bitcast(I32), 0)
+
+        nc.scalar.activation(out=dummy[:], in_=dummy[:], func=ACT.Sigmoid)
+        nc.scalar.dma_start(out=bias_rows[0:NB, :], in_=b_bb.rearrange("(c p) -> c p", p=P))
+        nc.scalar.dma_start(out=bias_rows[NB : 2 * NB, :], in_=b_rf.rearrange("(c p) -> c p", p=P))
+
+        def load_planes(pl, scales):
+            for q in range(4):
+                nc.sync.dma_start(out=pl[32 * q : 32 * q + 4, :, :].bitcast(I32), in_=scales[:, 4 * q : 4 * q + 4, :].rearrange("g r n -> r g n").bitcast(I32))
+
+        w_groups = []
+
+        def load_w(c0, n):
+            t = keep.tile([P, GB, n * 256], U8, name="w_%d" % c0, align_bytes=64)
+            nc.sync.dma_start(out=t[:], in_=w_words[:, :, 256 * c0 : 256 * (c0 + n)].rearrange("g p n -> p g n"))
+            w_groups.append((c0, n, t))
+
+        bb_t = []
+
+        def load_bb(t):
+            x = keep.tile([P, GB, 1024], U8, name="bb_%d" % t, align_bytes=64)
+            nc.sync.dma_start(out=x[:], in_=bb_words[:, :, 1024 * t : 1024 * (t + 1)].rearrange("g p n -> p g n"))
+            bb_t.append(x)
+
+        load_w(0, 1)
+        load_bb(0)
+        load_planes(w_pl, w_scales)
+        load_planes(bb_pl, bb_scales)
+        for t in range(1, NT):
+            load_bb(t)
+        load_w(1, 3)
+        load_w(4, 4)
+        load_w(8, 4)
+        load_planes(rf_pl, rf_scales)
+        load_planes(wr_pl, wr_scales)
+        rf_w = keep.tile([P, GR, 2 * B], U8, name="rf_w", align_bytes=64)
+        nc.sync.dma_start(out=rf_w[:], in_=rf_words.rearrange("g p n -> p g n"))
+        wr_w = []
+        for g in range(0, GR, 2):
+            x = keep.tile([P, 2, 2 * DB], U8, name="wr_%d" % g, align_bytes=64)
+            nc.sync.dma_start(out=x[:], in_=wr_words[g : g + 2, :, :].rearrange("g p n -> p g n"))
+            wr_w.append(x)
+
+        bias_ps = ptr.tile([P, P], BF16, name="tr")
+        nc.tensor.transpose(bias_ps[:], bias_rows[:], ident_b[:])
+        nc.vector.tensor_copy(out=bias[:], in_=bias_ps[:, 0 : 2 * NB])
+        nc.vector.tensor_scalar(out=negb[:], in0=bias[:, 0:2], scalar1=-1.0, scalar2=None, op0=ALU.mult)
+
+        ys, ts = {}, {}
+
+        def mx_bank(u, t):
+            ps = pmx.tile([P, 512], F32, name="mx")
+            if u == "R":
+                for k in range(4):
+                    c = 4 * t + k
+                    for g in range(GR):
+                        nc.tensor.matmul_mx(
+                            out=ps[:, P * k : P * (k + 1)],
+                            lhsT=wr_w[g // 2][:, g % 2, 256 * c : 256 * (c + 1)].bitcast(FP4),
+                            lhsT_scale=wr_pl[:, g, P * c : P * (c + 1)],
+                            rhs=rf_w[:, g, :].bitcast(FP4),
+                            rhs_scale=rf_pl[:, g, :],
+                            start=(g == 0),
+                            stop=(g == GR - 1),
+                        )
+                y = ys[u]
+                nc.vector.tensor_tensor(
+                    out=y[:, 512 * t : 512 * (t + 1)].rearrange("p (c b) -> p c b", b=B),
+                    in0=ps[:].rearrange("p (c b) -> p c b", b=B),
+                    in1=bias[:, NB + 4 * t : NB + 4 * (t + 1)].unsqueeze(2).to_broadcast([P, 4, B]),
+                    op=ALU.add,
+                )
+                return
+            for c0, n, wt in w_groups:
+                if c0 <= u < c0 + n:
+                    wcol, wtile = u - c0, wt
+            for g in range(GB):
+                nc.tensor.matmul_mx(
+                    out=ps[:],
+                    lhsT=wtile[:, g, 256 * wcol : 256 * (wcol + 1)].bitcast(FP4),
+                    lhsT_scale=w_pl[:, g, P * u : P * (u + 1)],
+                    rhs=bb_t[t][:, g, :].bitcast(FP4),
+                    rhs_scale=bb_pl[:, g, 512 * t : 512 * (t + 1)],
+                    start=(g == 0),
+                    stop=(g == GB - 1),
+                )
+            y = ys[u]
+            if u in (0, 1):
+                nc.scalar.activation(
+                    out=ts[u][:].rearrange("p (j b) -> p j b", b=B)[:, :, BQ * t : BQ * (t + 1)],
+                    in_=ps[:].rearrange("p (b j) -> p j b", j=G),
+                    func=ACT.Sigmoid,
+                    scale=-1.0,
+                    bias=negb[:, u : u + 1],
+                )
+            nc.vector.tensor_scalar(
+                out=y[:].rearrange("p (j b) -> p j b", b=B)[:, :, BQ * t : BQ * (t + 1)],
+                in0=ps[:].rearrange("p (b j) -> p j b", j=G),
+                scalar1=bias[:, u : u + 1],
+                scalar2=None,
+                op0=ALU.add,
+            )
+
+        def banks(u):
+            return 3 if u == "R" else NT
+
+        def width(u):
+            return DB if u == "R" else TOK
+
+        def fill(units):
+            for u in units:
+                ys[u] = ypool.tile([P, TOK], F32, name="y")
+            for i in range(0, len(units), 2):
+                pair = units[i : i + 2]
+                for t in range(NT):
+                    for u in pair:
+                        if t < banks(u):
+                            mx_bank(u, t)
+
+        def sig(u):
+            ts[u] = tpool.tile([P, TOK], F32, name="t")
+            n = width(u)
+            nc.scalar.activation(out=ts[u][:, 0:n], in_=ys[u][:, 0:n], func=ACT.Sigmoid, scale=-1.0)
+
+        def log(u):
+            n = width(u)
+            nc.scalar.activation(out=ts[u][:, 0:n], in_=ts[u][:, 0:n], func=ACT.Ln, bias=tiny[:])
+
+        def tanh_mult(u):
+            n = width(u)
+            t = ts[u]
+            nc.scalar.activation(out=t[:, 0:n], in_=t[:, 0:n], func=ACT.Tanh, scale=-1.0)
+            eng = nc.gpsimd if u in GPS_MULT else nc.vector
+            eng.tensor_tensor(out=t[:, 0:n], in0=ys[u][:, 0:n], in1=t[:, 0:n], op=ALU.mult)
+
+        def square(eng, u):
+            t = ts[u]
+            eng.tensor_tensor(out=t[:], in0=t[:], in1=t[:], op=ALU.mult)
+
+        def ars(u, lo=0, hi=TOK):
+            t = ts[u]
+            nc.scalar.activation(out=t[:, lo:hi], in_=t[:, lo:hi], func=ACT.Abs_reciprocal_sqrt, scale=0.5, bias=half[:])
+
+        def ars_mult(u, lo=0, hi=TOK):
+            t = ts[u]
+            nc.vector.scalar_tensor_tensor(out=t[:, lo:hi], in0=t[:, lo:hi], scalar=1.0, in1=ys[u][:, lo:hi], op0=ALU.subtract, op1=ALU.mult)
+
+        def finish(u):
+            t = ts[u]
+            if u == "R":
+                for k in range(3):
+                    ps = ptr.tile([P, 512], F32, name="tr")
+                    for i in range(4):
+                        nc.tensor.transpose(ps[:, P * i : P * (i + 1)], t[:, 512 * k + P * i : 512 * k + P * (i + 1)], ident[:])
+                    nc.vector.tensor_copy(out=r_tok[:, 512 * k : 512 * (k + 1)], in_=ps[:])
+                return
+            o = opool.tile([P, G, P], F32, name="o")
+            for k in range(4):
+                ps = ptr.tile([P, 512], F32, name="tr")
+                for i in range(4):
+                    j = 4 * k + i
+                    nc.tensor.transpose(ps[:, P * i : P * (i + 1)], t[:, P * j : P * (j + 1)], ident[:])
+                nc.vector.tensor_tensor(
+                    out=o[:, 4 * k : 4 * (k + 1), :],
+                    in0=ps[:].rearrange("p (j c) -> p j c", c=P),
+                    in1=r_tok[:, P * u : P * (u + 1)].unsqueeze(1).to_broadcast([P, 4, P]),
+                    op=ALU.add,
+                )
+                if k % 2 == 1:
+                    js = slice(4 * (k - 1), 4 * (k + 1))
+                    nc.sync.dma_start(out=out[:, js, P * u : P * (u + 1)], in_=o[:, js, :])
+
+        for u in (0, 1):
+            ys[u] = ypool.tile([P, TOK], F32, name="y")
+            ts[u] = tpool.tile([P, TOK], F32, name="t")
+            for t in range(NT):
+                mx_bank(u, t)
+            if u == 1:
+                square(nc.vector, 0)
+        square(nc.vector, 1)
+        fill([2, 3])
+        fill([4, "R"])
+        for u in (0, 1):
+            ars(u)
+            square(nc.gpsimd, u)
+        for u in (2, 3, 4):
+            sig(u)
+        fill([5])
+        sig("R")
+        sig(5)
+        for u in (0, 1):
+            ars_mult(u)
+
+        fill([6, 7, 8, 9])
+        for u in ("R", 2, 3, 4, 5):
+            log(u)
+        tanh_mult("R")
+        tanh_mult(2)
+        finish("R")
+        sig(6)
+        square(nc.gpsimd, 6)
+        tanh_mult(3)
+        finish(0)
+        fill([10])
+        sig(7)
+        square(nc.gpsimd, 7)
+        tanh_mult(4)
+        finish(1)
+        finish(2)
+        fill([11])
+        sig(8)
+        square(nc.gpsimd, 8)
+        tanh_mult(5)
+        sig(9)
+        square(nc.gpsimd, 9)
+        finish(3)
+        sig(10)
+        square(nc.gpsimd, 10)
+        finish(4)
+        sig(11)
+        square(nc.gpsimd, 11)
+
+        prev = 5
+        for u in (6, 7, 8, 9, 10, 11):
+            for h in (0, 1):
+                lo, hi = h * TOK // 2, (h + 1) * TOK // 2
+                ars(u, lo, hi)
+                nc.scalar.activation(out=ts[u][:, lo:hi], in_=ts[u][:, lo:hi], func=ACT.Square)
+                ars_mult(u, lo, hi)
+            finish(prev)
+            prev = u
+        finish(prev)

@@ -18,22 +18,22 @@ NB = DB // P
 TOK = B * G
 NT = TOK // 512
 BQ = 512 // G
+HALF = TOK // 2
 FLOPS = 2 * TOK * DB * DB + 2 * B * DR * DB
 TINY = 1e-18
-
-GPS_MULT = {2, 4, 5}
+R = "R"
 
 
 def tile_gnn_layer_pb_kernel(tc, bb_words, bb_scales, rf_words, rf_scales, w_words, w_scales, b_bb, wr_words, wr_scales, b_rf, out):
     nc = tc.nc
     with ExitStack() as ctx:
         keep = ctx.enter_context(tc.tile_pool(name="keep", bufs=1))
-        ypool = ctx.enter_context(tc.tile_pool(name="ypool", bufs=9))
+        ypool = ctx.enter_context(tc.tile_pool(name="ypool", bufs=8))
         tpool = ctx.enter_context(tc.tile_pool(name="tpool", bufs=9))
         opool = ctx.enter_context(tc.tile_pool(name="opool", bufs=2))
-        pmx = ctx.enter_context(tc.psum_pool(name="pmx", bufs=4))
-        ptr = ctx.enter_context(tc.psum_pool(name="ptr", bufs=4))
-        ctx.enter_context(tc.manual_schedule())
+        pmx = ctx.enter_context(tc.psum_pool(name="pmx", bufs=5))
+        ptr = ctx.enter_context(tc.psum_pool(name="ptr", bufs=3))
+        ctx.enter_context(tc.manual_schedule(engines={mybir.EngineType.Activation, mybir.EngineType.SP}))
 
         dummy = keep.tile([P, 1], F32, name="dummy")
         w_pl = keep.tile([P, GB, DB], U8, name="w_pl", align_bytes=64)
@@ -42,12 +42,13 @@ def tile_gnn_layer_pb_kernel(tc, bb_words, bb_scales, rf_words, rf_scales, w_wor
         wr_pl = keep.tile([P, GR, DB], U8, name="wr_pl", align_bytes=64)
         bias_rows = keep.tile([P, P], BF16, name="bias_rows")
         bias = keep.tile([P, 2 * NB], F32, name="bias")
-        negb = keep.tile([P, 2], F32, name="negb")
+        negb = keep.tile([P, NB], F32, name="negb")
         tiny = keep.tile([P, 1], F32, name="tiny")
         half = keep.tile([P, 1], F32, name="half")
         ident_b = keep.tile([P, P], BF16, name="ident_b")
         ident = keep.tile([P, P], F32, name="ident")
         r_tok = keep.tile([P, DB], F32, name="r_tok")
+        r_ch = keep.tile([P, DB], F32, name="r_ch")
 
         nc.vector.memset(w_pl[:].bitcast(I32), 0)
         nc.vector.memset(bb_pl[:].bitcast(I32), 0)
@@ -56,9 +57,9 @@ def tile_gnn_layer_pb_kernel(tc, bb_words, bb_scales, rf_words, rf_scales, w_wor
         nc.gpsimd.memset(tiny[:], TINY)
         nc.gpsimd.memset(half[:], 0.5)
         make_identity(nc, ident_b[:])
+        nc.gpsimd.memset(rf_pl[:].bitcast(I32), 0)
+        nc.gpsimd.memset(wr_pl[:].bitcast(I32), 0)
         make_identity(nc, ident[:])
-        nc.vector.memset(rf_pl[:].bitcast(I32), 0)
-        nc.vector.memset(wr_pl[:].bitcast(I32), 0)
 
         nc.scalar.activation(out=dummy[:], in_=dummy[:], func=ACT.Sigmoid)
         nc.scalar.dma_start(out=bias_rows[0:NB, :], in_=b_bb.rearrange("(c p) -> c p", p=P))
@@ -68,12 +69,13 @@ def tile_gnn_layer_pb_kernel(tc, bb_words, bb_scales, rf_words, rf_scales, w_wor
             for q in range(4):
                 nc.sync.dma_start(out=pl[32 * q : 32 * q + 4, :, :].bitcast(I32), in_=scales[:, 4 * q : 4 * q + 4, :].rearrange("g r n -> r g n").bitcast(I32))
 
-        w_groups = []
+        w_tiles = {}
 
         def load_w(c0, n):
-            t = keep.tile([P, GB, n * 256], U8, name="w_%d" % c0, align_bytes=64)
-            nc.sync.dma_start(out=t[:], in_=w_words[:, :, 256 * c0 : 256 * (c0 + n)].rearrange("g p n -> p g n"))
-            w_groups.append((c0, n, t))
+            x = keep.tile([P, GB, n * 256], U8, name="w_%d" % c0, align_bytes=64)
+            nc.sync.dma_start(out=x[:], in_=w_words[:, :, 256 * c0 : 256 * (c0 + n)].rearrange("g p n -> p g n"))
+            for c in range(n):
+                w_tiles[c0 + c] = x[:, :, 256 * c : 256 * (c + 1)]
 
         bb_t = []
 
@@ -86,31 +88,72 @@ def tile_gnn_layer_pb_kernel(tc, bb_words, bb_scales, rf_words, rf_scales, w_wor
         load_bb(0)
         load_planes(w_pl, w_scales)
         load_planes(bb_pl, bb_scales)
-        for t in range(1, NT):
-            load_bb(t)
+        load_bb(1)
+        load_bb(2)
+        load_bb(3)
         load_w(1, 3)
-        load_w(4, 4)
-        load_w(8, 4)
-        load_planes(rf_pl, rf_scales)
-        load_planes(wr_pl, wr_scales)
         rf_w = keep.tile([P, GR, 2 * B], U8, name="rf_w", align_bytes=64)
         nc.sync.dma_start(out=rf_w[:], in_=rf_words.rearrange("g p n -> p g n"))
+        load_planes(rf_pl, rf_scales)
+        load_planes(wr_pl, wr_scales)
         wr_w = []
         for g in range(0, GR, 2):
             x = keep.tile([P, 2, 2 * DB], U8, name="wr_%d" % g, align_bytes=64)
             nc.sync.dma_start(out=x[:], in_=wr_words[g : g + 2, :, :].rearrange("g p n -> p g n"))
             wr_w.append(x)
+        load_w(4, 4)
+        load_w(8, 4)
 
         bias_ps = ptr.tile([P, P], BF16, name="tr")
         nc.tensor.transpose(bias_ps[:], bias_rows[:], ident_b[:])
         nc.vector.tensor_copy(out=bias[:], in_=bias_ps[:, 0 : 2 * NB])
-        nc.vector.tensor_scalar(out=negb[:], in0=bias[:, 0:2], scalar1=-1.0, scalar2=None, op0=ALU.mult)
+        nc.vector.tensor_scalar(out=negb[:], in0=bias[:, 0:NB], scalar1=-1.0, scalar2=None, op0=ALU.mult)
 
         ys, ts = {}, {}
 
-        def mx_bank(u, t):
+        def width(u):
+            return DB if u == R else TOK
+
+        def new_t(u):
+            if u == R:
+                ts[u] = r_ch
+            else:
+                ts[u] = tpool.tile([P, TOK], F32, name="t")
+
+        def product(u, t):
             ps = pmx.tile([P, 512], F32, name="mx")
-            if u == "R":
+            for g in range(GB):
+                nc.tensor.matmul_mx(
+                    out=ps[:],
+                    lhsT=w_tiles[u][:, g, :].bitcast(FP4),
+                    lhsT_scale=w_pl[:, g, P * u : P * (u + 1)],
+                    rhs=bb_t[t][:, g, :].bitcast(FP4),
+                    rhs_scale=bb_pl[:, g, 512 * t : 512 * (t + 1)],
+                    start=(g == 0),
+                    stop=(g == GB - 1),
+                )
+            return ps[:].rearrange("p (b j) -> p j b", j=G)
+
+        def part(x, t):
+            return x[:].rearrange("p (j b) -> p j b", b=B)[:, :, BQ * t : BQ * (t + 1)]
+
+        def fill(u, y=True, sig=False, banks=range(NT)):
+            if u not in ys and y:
+                ys[u] = ypool.tile([P, TOK], F32, name="y")
+            if u not in ts and sig:
+                new_t(u)
+            for t in banks:
+                v = product(u, t)
+                if sig:
+                    nc.scalar.activation(out=part(ts[u], t), in_=v, func=ACT.Sigmoid, scale=-1.0, bias=negb[:, u : u + 1])
+                if y:
+                    nc.vector.tensor_scalar(out=part(ys[u], t), in0=v, scalar1=bias[:, u : u + 1], scalar2=None, op0=ALU.add)
+
+        def fill_r():
+            y = ypool.tile([P, TOK], F32, name="y")
+            ys[R] = y
+            for t in range(3):
+                ps = pmx.tile([P, 512], F32, name="mx")
                 for k in range(4):
                     c = 4 * t + k
                     for g in range(GR):
@@ -123,170 +166,153 @@ def tile_gnn_layer_pb_kernel(tc, bb_words, bb_scales, rf_words, rf_scales, w_wor
                             start=(g == 0),
                             stop=(g == GR - 1),
                         )
-                y = ys[u]
                 nc.vector.tensor_tensor(
                     out=y[:, 512 * t : 512 * (t + 1)].rearrange("p (c b) -> p c b", b=B),
                     in0=ps[:].rearrange("p (c b) -> p c b", b=B),
                     in1=bias[:, NB + 4 * t : NB + 4 * (t + 1)].unsqueeze(2).to_broadcast([P, 4, B]),
                     op=ALU.add,
                 )
-                return
-            for c0, n, wt in w_groups:
-                if c0 <= u < c0 + n:
-                    wcol, wtile = u - c0, wt
-            for g in range(GB):
-                nc.tensor.matmul_mx(
-                    out=ps[:],
-                    lhsT=wtile[:, g, 256 * wcol : 256 * (wcol + 1)].bitcast(FP4),
-                    lhsT_scale=w_pl[:, g, P * u : P * (u + 1)],
-                    rhs=bb_t[t][:, g, :].bitcast(FP4),
-                    rhs_scale=bb_pl[:, g, 512 * t : 512 * (t + 1)],
-                    start=(g == 0),
-                    stop=(g == GB - 1),
-                )
-            y = ys[u]
-            if u in (0, 1):
-                nc.scalar.activation(
-                    out=ts[u][:].rearrange("p (j b) -> p j b", b=B)[:, :, BQ * t : BQ * (t + 1)],
-                    in_=ps[:].rearrange("p (b j) -> p j b", j=G),
-                    func=ACT.Sigmoid,
-                    scale=-1.0,
-                    bias=negb[:, u : u + 1],
-                )
-            nc.vector.tensor_scalar(
-                out=y[:].rearrange("p (j b) -> p j b", b=B)[:, :, BQ * t : BQ * (t + 1)],
-                in0=ps[:].rearrange("p (b j) -> p j b", j=G),
-                scalar1=bias[:, u : u + 1],
-                scalar2=None,
-                op0=ALU.add,
-            )
-
-        def banks(u):
-            return 3 if u == "R" else NT
-
-        def width(u):
-            return DB if u == "R" else TOK
-
-        def fill(units):
-            for u in units:
-                ys[u] = ypool.tile([P, TOK], F32, name="y")
-            for i in range(0, len(units), 2):
-                pair = units[i : i + 2]
-                for t in range(NT):
-                    for u in pair:
-                        if t < banks(u):
-                            mx_bank(u, t)
 
         def sig(u):
-            ts[u] = tpool.tile([P, TOK], F32, name="t")
+            new_t(u)
             n = width(u)
             nc.scalar.activation(out=ts[u][:, 0:n], in_=ys[u][:, 0:n], func=ACT.Sigmoid, scale=-1.0)
 
         def log(u):
-            n = width(u)
-            nc.scalar.activation(out=ts[u][:, 0:n], in_=ts[u][:, 0:n], func=ACT.Ln, bias=tiny[:])
+            nc.scalar.activation(out=ts[u][:], in_=ts[u][:], func=ACT.Ln, bias=tiny[:])
 
-        def tanh_mult(u):
-            n = width(u)
-            t = ts[u]
-            nc.scalar.activation(out=t[:, 0:n], in_=t[:, 0:n], func=ACT.Tanh, scale=-1.0)
-            eng = nc.gpsimd if u in GPS_MULT else nc.vector
-            eng.tensor_tensor(out=t[:, 0:n], in0=ys[u][:, 0:n], in1=t[:, 0:n], op=ALU.mult)
+        def tanh(u):
+            nc.scalar.activation(out=ts[u][:], in_=ts[u][:], func=ACT.Tanh, scale=-1.0)
 
-        def square(eng, u):
-            t = ts[u]
-            eng.tensor_tensor(out=t[:], in0=t[:], in1=t[:], op=ALU.mult)
+        def square(eng, u, lo=0, hi=None, step=512):
+            hi = width(u) if hi is None else hi
+            for a in range(lo, hi, step):
+                v = ts[u][:, a : min(a + step, hi)]
+                eng.tensor_tensor(out=v, in0=v, in1=v, op=ALU.mult)
 
-        def ars(u, lo=0, hi=TOK):
-            t = ts[u]
-            nc.scalar.activation(out=t[:, lo:hi], in_=t[:, lo:hi], func=ACT.Abs_reciprocal_sqrt, scale=0.5, bias=half[:])
+        def ssquare(u, h):
+            v = ts[u][:, HALF * h : HALF * (h + 1)]
+            nc.scalar.activation(out=v, in_=v, func=ACT.Square)
 
-        def ars_mult(u, lo=0, hi=TOK):
-            t = ts[u]
-            nc.vector.scalar_tensor_tensor(out=t[:, lo:hi], in0=t[:, lo:hi], scalar=1.0, in1=ys[u][:, lo:hi], op0=ALU.subtract, op1=ALU.mult)
+        def ars(u, lo, hi):
+            v = ts[u][:, lo:hi]
+            nc.scalar.activation(out=v, in_=v, func=ACT.Abs_reciprocal_sqrt, scale=0.5, bias=half[:])
 
-        def finish(u):
+        def ars_mult(u, lo, hi):
+            nc.vector.scalar_tensor_tensor(out=ts[u][:, lo:hi], in0=ts[u][:, lo:hi], scalar=1.0, in1=ys[u][:, lo:hi], op0=ALU.subtract, op1=ALU.mult)
+
+        def mult(eng, u, lo=0, hi=TOK):
+            eng.tensor_tensor(out=ts[u][:, lo:hi], in0=ys[u][:, lo:hi], in1=ts[u][:, lo:hi], op=ALU.mult)
+
+        def again_mult(u, banks=range(NT)):
+            for t in banks:
+                v = product(u, t)
+                nc.vector.scalar_tensor_tensor(out=part(ts[u], t), in0=v, scalar=bias[:, u : u + 1], in1=part(ts[u], t), op0=ALU.add, op1=ALU.mult)
+
+        o_tiles = {}
+
+        def finish(u, ks=range(4), on_scalar=()):
             t = ts[u]
-            if u == "R":
+            if u == R:
                 for k in range(3):
                     ps = ptr.tile([P, 512], F32, name="tr")
                     for i in range(4):
                         nc.tensor.transpose(ps[:, P * i : P * (i + 1)], t[:, 512 * k + P * i : 512 * k + P * (i + 1)], ident[:])
                     nc.vector.tensor_copy(out=r_tok[:, 512 * k : 512 * (k + 1)], in_=ps[:])
                 return
-            o = opool.tile([P, G, P], F32, name="o")
-            for k in range(4):
+            if u not in o_tiles:
+                o_tiles[u] = opool.tile([P, G, P], F32, name="o")
+            o = o_tiles[u]
+            for k in ks:
                 ps = ptr.tile([P, 512], F32, name="tr")
                 for i in range(4):
                     j = 4 * k + i
-                    nc.tensor.transpose(ps[:, P * i : P * (i + 1)], t[:, P * j : P * (j + 1)], ident[:])
-                nc.vector.tensor_tensor(
-                    out=o[:, 4 * k : 4 * (k + 1), :],
-                    in0=ps[:].rearrange("p (j c) -> p j c", c=P),
-                    in1=r_tok[:, P * u : P * (u + 1)].unsqueeze(1).to_broadcast([P, 4, P]),
-                    op=ALU.add,
-                )
+                    v = ps[:, P * i : P * (i + 1)]
+                    if k in on_scalar:
+                        nc.tensor.matmul(v, lhsT=t[:, P * j : P * (j + 1)], rhs=ident[:], is_transpose=True, start=True, stop=False)
+                        nc.tensor.matmul(v, lhsT=r_ch[:, P * u : P * (u + 1)], rhs=ident[:], is_transpose=True, start=False, stop=True)
+                    else:
+                        nc.tensor.transpose(v, t[:, P * j : P * (j + 1)], ident[:])
+                dst = o[:, 4 * k : 4 * (k + 1), :]
+                src = ps[:].rearrange("p (j c) -> p j c", c=P)
+                if k in on_scalar:
+                    nc.scalar.copy(out=dst, in_=src)
+                else:
+                    nc.vector.tensor_tensor(out=dst, in0=src, in1=r_tok[:, P * u : P * (u + 1)].unsqueeze(1).to_broadcast([P, 4, P]), op=ALU.add)
                 if k % 2 == 1:
                     js = slice(4 * (k - 1), 4 * (k + 1))
                     nc.sync.dma_start(out=out[:, js, P * u : P * (u + 1)], in_=o[:, js, :])
 
-        for u in (0, 1):
-            ys[u] = ypool.tile([P, TOK], F32, name="y")
-            ts[u] = tpool.tile([P, TOK], F32, name="t")
-            for t in range(NT):
-                mx_bank(u, t)
-            if u == 1:
-                square(nc.vector, 0)
-        square(nc.vector, 1)
-        fill([2, 3])
-        fill([4, "R"])
-        for u in (0, 1):
-            ars(u)
+        for u in (0, 1, 2):
+            fill(u, sig=True)
             square(nc.gpsimd, u)
-        for u in (2, 3, 4):
-            sig(u)
-        fill([5])
-        sig("R")
-        sig(5)
+        fill_r()
+        sig(R)
+        square(nc.vector, R, step=DB)
+        for lo, hi in ((0, 1024), (1024, DB)):
+            ars(R, lo, hi)
+            square(nc.vector, R, lo, hi, step=1024)
+            ars_mult(R, lo, hi)
         for u in (0, 1):
-            ars_mult(u)
-
-        fill([6, 7, 8, 9])
-        for u in ("R", 2, 3, 4, 5):
-            log(u)
-        tanh_mult("R")
-        tanh_mult(2)
-        finish("R")
-        sig(6)
-        square(nc.gpsimd, 6)
-        tanh_mult(3)
+            for h in (0, 1):
+                ars(u, HALF * h, HALF * (h + 1))
+        fill(3)
+        for h in (0, 1):
+            ars(2, HALF * h, HALF * (h + 1))
+        fill(4)
+        finish(R)
+        for u in (0, 1, 2):
+            for h in (0, 1):
+                square(nc.gpsimd, u, HALF * h, HALF * (h + 1))
+        sig(3)
+        ars_mult(0, 0, HALF)
+        ars_mult(0, HALF, TOK)
+        sig(4)
+        fill(5, y=False, sig=True)
         finish(0)
-        fill([10])
-        sig(7)
-        square(nc.gpsimd, 7)
-        tanh_mult(4)
+        fill(6, y=False, sig=True)
+        ars_mult(1, 0, HALF)
+        ars_mult(1, HALF, TOK)
         finish(1)
+        fill(7, y=False, sig=True)
+        ars_mult(2, 0, HALF)
+        ars_mult(2, HALF, TOK)
         finish(2)
-        fill([11])
+        for u in (3, 4, 5, 6, 7):
+            log(u)
+        for u in (8, 9, 10, 11):
+            fill(u)
+        tanh(3)
+        mult(nc.vector, 3)
         sig(8)
         square(nc.gpsimd, 8)
-        tanh_mult(5)
+        tanh(4)
+        finish(3)
+        mult(nc.vector, 4)
         sig(9)
         square(nc.gpsimd, 9)
-        finish(3)
+        tanh(5)
+        finish(4)
+        again_mult(5)
         sig(10)
         square(nc.gpsimd, 10)
-        finish(4)
+        tanh(6)
+        finish(5)
+        again_mult(6)
         sig(11)
         square(nc.gpsimd, 11)
-
-        prev = 5
-        for u in (6, 7, 8, 9, 10, 11):
+        tanh(7)
+        finish(6)
+        again_mult(7)
+        for u in (8, 9, 10, 11):
             for h in (0, 1):
-                lo, hi = h * TOK // 2, (h + 1) * TOK // 2
-                ars(u, lo, hi)
-                nc.scalar.activation(out=ts[u][:, lo:hi], in_=ts[u][:, lo:hi], func=ACT.Square)
-                ars_mult(u, lo, hi)
-            finish(prev)
-            prev = u
-        finish(prev)
+                ars(u, HALF * h, HALF * (h + 1))
+                ssquare(u, h)
+        finish(7)
+        for u in (8, 9, 10, 11):
+            for h in (0, 1):
+                ars_mult(u, HALF * h, HALF * (h + 1))
+                if u >= 10:
+                    finish(u, (2 * h, 2 * h + 1), on_scalar=(1, 3))
+                else:
+                    finish(u, (2 * h, 2 * h + 1))

@@ -36,8 +36,13 @@ def tile_gnn_layer_pb_kernel(tc, bb_words, bb_scales, rf_words, rf_scales, w_wor
         ctx.enter_context(tc.manual_schedule(engines={mybir.EngineType.Activation, mybir.EngineType.SP}))
 
         dummy = keep.tile([P, 1], F32, name="dummy")
-        w_pl = keep.tile([P, GB, DB], U8, name="w_pl", align_bytes=64)
-        bb_pl = keep.tile([P, GB, TOK], U8, name="bb_pl", align_bytes=64)
+        w_pl = []
+        for n in (512, 1024):
+            x = keep.tile([P, GB, n], U8, name="w_pl%d" % n, align_bytes=64)
+            w_pl.append(x)
+        bb_pl0 = keep.tile([P, GB, HALF], U8, name="bb_pl0", align_bytes=64)
+        bb_pl1 = keep.tile([P, GB, HALF], U8, name="bb_pl1", align_bytes=64)
+        bb_pl = (bb_pl0, bb_pl1)
         rf_pl = keep.tile([P, GR, B], U8, name="rf_pl", align_bytes=64)
         wr_pl = keep.tile([P, GR, DB], U8, name="wr_pl", align_bytes=64)
         bias_rows = keep.tile([P, P], BF16, name="bias_rows")
@@ -50,8 +55,8 @@ def tile_gnn_layer_pb_kernel(tc, bb_words, bb_scales, rf_words, rf_scales, w_wor
         r_tok = keep.tile([P, DB], F32, name="r_tok")
         r_ch = keep.tile([P, DB], F32, name="r_ch")
 
-        nc.vector.memset(w_pl[:].bitcast(I32), 0)
-        nc.vector.memset(bb_pl[:].bitcast(I32), 0)
+        for x in (w_pl[0], bb_pl[0], bb_pl[1], w_pl[1]):
+            nc.vector.memset(x[:].bitcast(I32), 0)
         nc.gpsimd.memset(dummy[:], 0.0)
         nc.gpsimd.memset(bias_rows[:], 0.0)
         nc.gpsimd.memset(tiny[:], TINY)
@@ -86,12 +91,15 @@ def tile_gnn_layer_pb_kernel(tc, bb_words, bb_scales, rf_words, rf_scales, w_wor
 
         load_w(0, 1)
         load_bb(0)
-        load_planes(w_pl, w_scales)
-        load_planes(bb_pl, bb_scales)
+        load_planes(w_pl[0], w_scales[:, :, 0:512])
+        load_planes(bb_pl[0], bb_scales[:, :, 0:HALF])
         load_bb(1)
+        load_planes(bb_pl[1], bb_scales[:, :, HALF:TOK])
         load_bb(2)
         load_bb(3)
         load_w(1, 3)
+        load_planes(w_pl[1], w_scales[:, :, 512:DB])
+        load_w(4, 4)
         rf_w = keep.tile([P, GR, 2 * B], U8, name="rf_w", align_bytes=64)
         nc.sync.dma_start(out=rf_w[:], in_=rf_words.rearrange("g p n -> p g n"))
         load_planes(rf_pl, rf_scales)
@@ -101,7 +109,6 @@ def tile_gnn_layer_pb_kernel(tc, bb_words, bb_scales, rf_words, rf_scales, w_wor
             x = keep.tile([P, 2, 2 * DB], U8, name="wr_%d" % g, align_bytes=64)
             nc.sync.dma_start(out=x[:], in_=wr_words[g : g + 2, :, :].rearrange("g p n -> p g n"))
             wr_w.append(x)
-        load_w(4, 4)
         load_w(8, 4)
 
         bias_ps = ptr.tile([P, P], BF16, name="tr")
@@ -122,13 +129,14 @@ def tile_gnn_layer_pb_kernel(tc, bb_words, bb_scales, rf_words, rf_scales, w_wor
 
         def product(u, t):
             ps = pmx.tile([P, 512], F32, name="mx")
+            wp, wo = (w_pl[0], P * u) if u < 4 else (w_pl[1], P * (u - 4))
             for g in range(GB):
                 nc.tensor.matmul_mx(
                     out=ps[:],
                     lhsT=w_tiles[u][:, g, :].bitcast(FP4),
-                    lhsT_scale=w_pl[:, g, P * u : P * (u + 1)],
+                    lhsT_scale=wp[:, g, wo : wo + P],
                     rhs=bb_t[t][:, g, :].bitcast(FP4),
-                    rhs_scale=bb_pl[:, g, 512 * t : 512 * (t + 1)],
+                    rhs_scale=bb_pl[t // 2][:, g, 512 * (t % 2) : 512 * (t % 2 + 1)],
                     start=(g == 0),
                     stop=(g == GB - 1),
                 )
@@ -178,11 +186,11 @@ def tile_gnn_layer_pb_kernel(tc, bb_words, bb_scales, rf_words, rf_scales, w_wor
             n = width(u)
             nc.scalar.activation(out=ts[u][:, 0:n], in_=ys[u][:, 0:n], func=ACT.Sigmoid, scale=-1.0)
 
-        def log(u):
-            nc.scalar.activation(out=ts[u][:], in_=ts[u][:], func=ACT.Ln, bias=tiny[:])
+        def log(u, n=TOK):
+            nc.scalar.activation(out=ts[u][:, 0:n], in_=ts[u][:, 0:n], func=ACT.Ln, bias=tiny[:])
 
-        def tanh(u):
-            nc.scalar.activation(out=ts[u][:], in_=ts[u][:], func=ACT.Tanh, scale=-1.0)
+        def tanh(u, n=TOK):
+            nc.scalar.activation(out=ts[u][:, 0:n], in_=ts[u][:, 0:n], func=ACT.Tanh, scale=-1.0)
 
         def square(eng, u, lo=0, hi=None, step=512):
             hi = width(u) if hi is None else hi
@@ -243,76 +251,98 @@ def tile_gnn_layer_pb_kernel(tc, bb_words, bb_scales, rf_words, rf_scales, w_wor
                     js = slice(4 * (k - 1), 4 * (k + 1))
                     nc.sync.dma_start(out=out[:, js, P * u : P * (u + 1)], in_=o[:, js, :])
 
-        for u in (0, 1, 2):
+        for u in (0, 1):
             fill(u, sig=True)
-            square(nc.gpsimd, u)
-        fill_r()
-        sig(R)
-        square(nc.vector, R, step=DB)
-        for lo, hi in ((0, 1024), (1024, DB)):
-            ars(R, lo, hi)
-            square(nc.vector, R, lo, hi, step=1024)
-            ars_mult(R, lo, hi)
+            square(nc.vector, u, step=HALF)
+        fill(2)
         for u in (0, 1):
             for h in (0, 1):
                 ars(u, HALF * h, HALF * (h + 1))
         fill(3)
-        for h in (0, 1):
-            ars(2, HALF * h, HALF * (h + 1))
-        fill(4)
-        finish(R)
-        for u in (0, 1, 2):
+        for u in (0, 1):
             for h in (0, 1):
-                square(nc.gpsimd, u, HALF * h, HALF * (h + 1))
+                square(nc.vector, u, HALF * h, HALF * (h + 1), step=HALF)
+                ars_mult(u, HALF * h, HALF * (h + 1))
+        sig(2)
         sig(3)
-        ars_mult(0, 0, HALF)
-        ars_mult(0, HALF, TOK)
-        sig(4)
+        fill(4, y=False, sig=True)
         fill(5, y=False, sig=True)
-        finish(0)
         fill(6, y=False, sig=True)
-        ars_mult(1, 0, HALF)
-        ars_mult(1, HALF, TOK)
-        finish(1)
-        fill(7, y=False, sig=True)
-        ars_mult(2, 0, HALF)
-        ars_mult(2, HALF, TOK)
-        finish(2)
-        for u in (3, 4, 5, 6, 7):
-            log(u)
-        for u in (8, 9, 10, 11):
-            fill(u)
+        fill_r()
+        sig(R)
+        fill(7)
+        fill(8)
+        fill(9)
+        fill(10)
+        fill(11)
+        log(R, DB)
+        log(2)
+        log(3)
+        log(4)
+        log(5)
+        log(6)
+        tanh(R, DB)
+        mult(nc.vector, R, 0, DB)
+        finish(R)
+        tanh(2)
+        mult(nc.vector, 2)
+        finish(0)
+        sig(7)
+        square(nc.gpsimd, 7)
         tanh(3)
-        mult(nc.vector, 3)
+        mult(nc.gpsimd, 3)
+        finish(1)
         sig(8)
         square(nc.gpsimd, 8)
         tanh(4)
-        finish(3)
-        mult(nc.vector, 4)
+        again_mult(4)
+        finish(2)
         sig(9)
         square(nc.gpsimd, 9)
         tanh(5)
-        finish(4)
         again_mult(5)
+        finish(3)
         sig(10)
         square(nc.gpsimd, 10)
         tanh(6)
-        finish(5)
         again_mult(6)
+        finish(4)
         sig(11)
         square(nc.gpsimd, 11)
-        tanh(7)
+        ars(7, 0, 1024)
+        ssquare(7, 0)
+        ars(7, 1024, 2048)
+        ssquare(7, 1)
+        finish(5)
+        ars_mult(7, 0, 1024)
+        ars_mult(7, 1024, 2048)
+        ars(8, 0, 1024)
+        ssquare(8, 0)
+        ars(8, 1024, 2048)
+        ssquare(8, 1)
         finish(6)
-        again_mult(7)
-        for u in (8, 9, 10, 11):
-            for h in (0, 1):
-                ars(u, HALF * h, HALF * (h + 1))
-                ssquare(u, h)
+        ars_mult(8, 0, 1024)
+        ars_mult(8, 1024, 2048)
+        ars(9, 0, 1024)
+        ssquare(9, 0)
+        ars(9, 1024, 2048)
+        ssquare(9, 1)
         finish(7)
-        for u in (8, 9, 10, 11):
-            for h in (0, 1):
-                ars_mult(u, HALF * h, HALF * (h + 1))
-                if u >= 10:
-                    finish(u, (2 * h, 2 * h + 1), on_scalar=(1, 3))
-                else:
-                    finish(u, (2 * h, 2 * h + 1))
+        ars_mult(9, 0, 1024)
+        ars_mult(9, 1024, 2048)
+        ars(10, 0, 1024)
+        ssquare(10, 0)
+        ars(10, 1024, 2048)
+        ssquare(10, 1)
+        finish(8)
+        ars_mult(10, 0, 1024)
+        ars_mult(10, 1024, 2048)
+        ars(11, 0, 1024)
+        ssquare(11, 0)
+        ars(11, 1024, 2048)
+        ssquare(11, 1)
+        finish(9)
+        ars_mult(11, 0, 1024)
+        ars_mult(11, 1024, 2048)
+        finish(10)
+        finish(11)

from contextlib import ExitStack

import concourse.mybir as mybir
from concourse.masks import make_identity

F32 = mybir.dt.float32
BF16 = mybir.dt.bfloat16
U8 = mybir.dt.uint8
I32 = mybir.dt.int32
FP4 = mybir.dt.float4_e2m1fn_x4
ACT = mybir.ActivationFunctionType
ALU = mybir.AluOpType

P = 128
B, G, DB, DR = 128, 16, 1536, 3072
GB, GR = DB // 512, DR // 512
NB = DB // P
TOK = B * G
NT = TOK // 512
BQ = 512 // G
HALF = TOK // 2
FLOPS = 2 * TOK * DB * DB + 2 * B * DR * DB
TINY = 1e-18
R = "R"


def tile_gnn_layer_pb_kernel(tc, bb_words, bb_scales, rf_words, rf_scales, w_words, w_scales, b_bb, wr_words, wr_scales, b_rf, out):
    nc = tc.nc
    with ExitStack() as ctx:
        keep = ctx.enter_context(tc.tile_pool(name="keep", bufs=1))
        ypool = ctx.enter_context(tc.tile_pool(name="ypool", bufs=8))
        tpool = ctx.enter_context(tc.tile_pool(name="tpool", bufs=9))
        opool = ctx.enter_context(tc.tile_pool(name="opool", bufs=2))
        pmx = ctx.enter_context(tc.psum_pool(name="pmx", bufs=5))
        ptr = ctx.enter_context(tc.psum_pool(name="ptr", bufs=3))
        ctx.enter_context(tc.manual_schedule(engines={mybir.EngineType.Activation, mybir.EngineType.SP}))

        dummy = keep.tile([P, 1], F32, name="dummy")
        w_pl = []
        for n in (512, 1024):
            x = keep.tile([P, GB, n], U8, name="w_pl%d" % n, align_bytes=64)
            w_pl.append(x)
        bb_pl0 = keep.tile([P, GB, HALF], U8, name="bb_pl0", align_bytes=64)
        bb_pl1 = keep.tile([P, GB, HALF], U8, name="bb_pl1", align_bytes=64)
        bb_pl = (bb_pl0, bb_pl1)
        rf_pl = keep.tile([P, GR, B], U8, name="rf_pl", align_bytes=64)
        wr_pl = keep.tile([P, GR, DB], U8, name="wr_pl", align_bytes=64)
        bias_rows = keep.tile([P, P], BF16, name="bias_rows")
        bias = keep.tile([P, 2 * NB], F32, name="bias")
        negb = keep.tile([P, NB], F32, name="negb")
        tiny = keep.tile([P, 1], F32, name="tiny")
        half = keep.tile([P, 1], F32, name="half")
        ident_b = keep.tile([P, P], BF16, name="ident_b")
        ident = keep.tile([P, P], F32, name="ident")
        r_tok = keep.tile([P, DB], F32, name="r_tok")
        r_ch = keep.tile([P, DB], F32, name="r_ch")

        for x in (w_pl[0], bb_pl[0], bb_pl[1], w_pl[1]):
            nc.vector.memset(x[:].bitcast(I32), 0)
        nc.gpsimd.memset(dummy[:], 0.0)
        nc.gpsimd.memset(bias_rows[:], 0.0)
        nc.gpsimd.memset(tiny[:], TINY)
        nc.gpsimd.memset(half[:], 0.5)
        make_identity(nc, ident_b[:])
        nc.gpsimd.memset(rf_pl[:].bitcast(I32), 0)
        nc.gpsimd.memset(wr_pl[:].bitcast(I32), 0)
        make_identity(nc, ident[:])

        nc.scalar.activation(out=dummy[:], in_=dummy[:], func=ACT.Sigmoid)
        nc.scalar.dma_start(out=bias_rows[0:NB, :], in_=b_bb.rearrange("(c p) -> c p", p=P))
        nc.scalar.dma_start(out=bias_rows[NB : 2 * NB, :], in_=b_rf.rearrange("(c p) -> c p", p=P))

        def load_planes(pl, scales):
            for q in range(4):
                nc.sync.dma_start(out=pl[32 * q : 32 * q + 4, :, :].bitcast(I32), in_=scales[:, 4 * q : 4 * q + 4, :].rearrange("g r n -> r g n").bitcast(I32))

        w_tiles = {}

        def load_w(c0, n):
            x = keep.tile([P, GB, n * 256], U8, name="w_%d" % c0, align_bytes=64)
            nc.sync.dma_start(out=x[:], in_=w_words[:, :, 256 * c0 : 256 * (c0 + n)].rearrange("g p n -> p g n"))
            for c in range(n):
                w_tiles[c0 + c] = x[:, :, 256 * c : 256 * (c + 1)]

        bb_t = []

        def load_bb(t):
            x = keep.tile([P, GB, 1024], U8, name="bb_%d" % t, align_bytes=64)
            nc.sync.dma_start(out=x[:], in_=bb_words[:, :, 1024 * t : 1024 * (t + 1)].rearrange("g p n -> p g n"))
            bb_t.append(x)

        load_w(0, 1)
        load_bb(0)
        load_planes(w_pl[0], w_scales[:, :, 0:512])
        load_planes(bb_pl[0], bb_scales[:, :, 0:HALF])
        load_bb(1)
        load_planes(bb_pl[1], bb_scales[:, :, HALF:TOK])
        load_bb(2)
        load_bb(3)
        load_w(1, 3)
        load_planes(w_pl[1], w_scales[:, :, 512:DB])
        load_w(4, 4)
        rf_w = keep.tile([P, GR, 2 * B], U8, name="rf_w", align_bytes=64)
        nc.sync.dma_start(out=rf_w[:], in_=rf_words.rearrange("g p n -> p g n"))
        load_planes(rf_pl, rf_scales)
        load_planes(wr_pl, wr_scales)
        wr_w = []
        for g in range(0, GR, 2):
            x = keep.tile([P, 2, 2 * DB], U8, name="wr_%d" % g, align_bytes=64)
            nc.sync.dma_start(out=x[:], in_=wr_words[g : g + 2, :, :].rearrange("g p n -> p g n"))
            wr_w.append(x)
        load_w(8, 4)

        bias_ps = ptr.tile([P, P], BF16, name="tr")
        nc.tensor.transpose(bias_ps[:], bias_rows[:], ident_b[:])
        nc.vector.tensor_copy(out=bias[:], in_=bias_ps[:, 0 : 2 * NB])
        nc.vector.tensor_scalar(out=negb[:], in0=bias[:, 0:NB], scalar1=-1.0, scalar2=None, op0=ALU.mult)

        ys, ts = {}, {}

        def width(u):
            return DB if u == R else TOK

        def new_t(u):
            if u == R:
                ts[u] = r_ch
            else:
                ts[u] = tpool.tile([P, TOK], F32, name="t")

        def product(u, t):
            ps = pmx.tile([P, 512], F32, name="mx")
            wp, wo = (w_pl[0], P * u) if u < 4 else (w_pl[1], P * (u - 4))
            for g in range(GB):
                nc.tensor.matmul_mx(
                    out=ps[:],
                    lhsT=w_tiles[u][:, g, :].bitcast(FP4),
                    lhsT_scale=wp[:, g, wo : wo + P],
                    rhs=bb_t[t][:, g, :].bitcast(FP4),
                    rhs_scale=bb_pl[t // 2][:, g, 512 * (t % 2) : 512 * (t % 2 + 1)],
                    start=(g == 0),
                    stop=(g == GB - 1),
                )
            return ps[:].rearrange("p (b j) -> p j b", j=G)

        def part(x, t):
            return x[:].rearrange("p (j b) -> p j b", b=B)[:, :, BQ * t : BQ * (t + 1)]

        def fill(u, y=True, sig=False, banks=range(NT)):
            if u not in ys and y:
                ys[u] = ypool.tile([P, TOK], F32, name="y")
            if u not in ts and sig:
                new_t(u)
            for t in banks:
                v = product(u, t)
                if sig:
                    nc.scalar.activation(out=part(ts[u], t), in_=v, func=ACT.Sigmoid, scale=-1.0, bias=negb[:, u : u + 1])
                if y:
                    nc.vector.tensor_scalar(out=part(ys[u], t), in0=v, scalar1=bias[:, u : u + 1], scalar2=None, op0=ALU.add)

        def fill_r():
            y = ypool.tile([P, TOK], F32, name="y")
            ys[R] = y
            for t in range(3):
                ps = pmx.tile([P, 512], F32, name="mx")
                for k in range(4):
                    c = 4 * t + k
                    for g in range(GR):
                        nc.tensor.matmul_mx(
                            out=ps[:, P * k : P * (k + 1)],
                            lhsT=wr_w[g // 2][:, g % 2, 256 * c : 256 * (c + 1)].bitcast(FP4),
                            lhsT_scale=wr_pl[:, g, P * c : P * (c + 1)],
                            rhs=rf_w[:, g, :].bitcast(FP4),
                            rhs_scale=rf_pl[:, g, :],
                            start=(g == 0),
                            stop=(g == GR - 1),
                        )
                nc.vector.tensor_tensor(
                    out=y[:, 512 * t : 512 * (t + 1)].rearrange("p (c b) -> p c b", b=B),
                    in0=ps[:].rearrange("p (c b) -> p c b", b=B),
                    in1=bias[:, NB + 4 * t : NB + 4 * (t + 1)].unsqueeze(2).to_broadcast([P, 4, B]),
                    op=ALU.add,
                )

        def sig(u):
            new_t(u)
            n = width(u)
            nc.scalar.activation(out=ts[u][:, 0:n], in_=ys[u][:, 0:n], func=ACT.Sigmoid, scale=-1.0)

        def log(u, n=TOK):
            nc.scalar.activation(out=ts[u][:, 0:n], in_=ts[u][:, 0:n], func=ACT.Ln, bias=tiny[:])

        def tanh(u, n=TOK):
            nc.scalar.activation(out=ts[u][:, 0:n], in_=ts[u][:, 0:n], func=ACT.Tanh, scale=-1.0)

        def square(eng, u, lo=0, hi=None, step=512):
            hi = width(u) if hi is None else hi
            for a in range(lo, hi, step):
                v = ts[u][:, a : min(a + step, hi)]
                eng.tensor_tensor(out=v, in0=v, in1=v, op=ALU.mult)

        def ssquare(u, h):
            v = ts[u][:, HALF * h : HALF * (h + 1)]
            nc.scalar.activation(out=v, in_=v, func=ACT.Square)

        def ars(u, lo, hi):
            v = ts[u][:, lo:hi]
            nc.scalar.activation(out=v, in_=v, func=ACT.Abs_reciprocal_sqrt, scale=0.5, bias=half[:])

        def ars_mult(u, lo, hi):
            nc.vector.scalar_tensor_tensor(out=ts[u][:, lo:hi], in0=ts[u][:, lo:hi], scalar=1.0, in1=ys[u][:, lo:hi], op0=ALU.subtract, op1=ALU.mult)

        def mult(eng, u, lo=0, hi=TOK):
            eng.tensor_tensor(out=ts[u][:, lo:hi], in0=ys[u][:, lo:hi], in1=ts[u][:, lo:hi], op=ALU.mult)

        def again_mult(u, banks=range(NT)):
            for t in banks:
                v = product(u, t)
                nc.vector.scalar_tensor_tensor(out=part(ts[u], t), in0=v, scalar=bias[:, u : u + 1], in1=part(ts[u], t), op0=ALU.add, op1=ALU.mult)

        o_tiles = {}

        def finish(u, ks=range(4), on_scalar=()):
            t = ts[u]
            if u == R:
                for k in range(3):
                    ps = ptr.tile([P, 512], F32, name="tr")
                    for i in range(4):
                        nc.tensor.transpose(ps[:, P * i : P * (i + 1)], t[:, 512 * k + P * i : 512 * k + P * (i + 1)], ident[:])
                    nc.vector.tensor_copy(out=r_tok[:, 512 * k : 512 * (k + 1)], in_=ps[:])
                return
            if u not in o_tiles:
                o_tiles[u] = opool.tile([P, G, P], F32, name="o")
            o = o_tiles[u]
            for k in ks:
                ps = ptr.tile([P, 512], F32, name="tr")
                for i in range(4):
                    j = 4 * k + i
                    v = ps[:, P * i : P * (i + 1)]
                    if k in on_scalar:
                        nc.tensor.matmul(v, lhsT=t[:, P * j : P * (j + 1)], rhs=ident[:], is_transpose=True, start=True, stop=False)
                        nc.tensor.matmul(v, lhsT=r_ch[:, P * u : P * (u + 1)], rhs=ident[:], is_transpose=True, start=False, stop=True)
                    else:
                        nc.tensor.transpose(v, t[:, P * j : P * (j + 1)], ident[:])
                dst = o[:, 4 * k : 4 * (k + 1), :]
                src = ps[:].rearrange("p (j c) -> p j c", c=P)
                if k in on_scalar:
                    nc.scalar.copy(out=dst, in_=src)
                else:
                    nc.vector.tensor_tensor(out=dst, in0=src, in1=r_tok[:, P * u : P * (u + 1)].unsqueeze(1).to_broadcast([P, 4, P]), op=ALU.add)
                if k % 2 == 1:
                    js = slice(4 * (k - 1), 4 * (k + 1))
                    nc.sync.dma_start(out=out[:, js, P * u : P * (u + 1)], in_=o[:, js, :])

        for u in (0, 1):
            fill(u, sig=True)
            square(nc.vector, u, step=HALF)
        fill(2)
        for u in (0, 1):
            for h in (0, 1):
                ars(u, HALF * h, HALF * (h + 1))
        fill(3)
        for u in (0, 1):
            for h in (0, 1):
                square(nc.vector, u, HALF * h, HALF * (h + 1), step=HALF)
                ars_mult(u, HALF * h, HALF * (h + 1))
        sig(2)
        sig(3)
        fill(4, y=False, sig=True)
        fill(5, y=False, sig=True)
        fill(6, y=False, sig=True)
        fill_r()
        sig(R)
        fill(7)
        fill(8)
        fill(9)
        fill(10)
        fill(11)
        log(R, DB)
        log(2)
        log(3)
        log(4)
        log(5)
        log(6)
        tanh(R, DB)
        mult(nc.vector, R, 0, DB)
        finish(R)
        tanh(2)
        mult(nc.vector, 2)
        finish(0)
        sig(7)
        square(nc.gpsimd, 7)
        tanh(3)
        mult(nc.gpsimd, 3)
        finish(1)
        sig(8)
        square(nc.gpsimd, 8)
        tanh(4)
        again_mult(4)
        finish(2)
        sig(9)
        square(nc.gpsimd, 9)
        tanh(5)
        again_mult(5)
        finish(3)
        sig(10)
        square(nc.gpsimd, 10)
        tanh(6)
        again_mult(6)
        finish(4)
        sig(11)
        square(nc.gpsimd, 11)
        ars(7, 0, 1024)
        ssquare(7, 0)
        ars(7, 1024, 2048)
        ssquare(7, 1)
        finish(5)
        ars_mult(7, 0, 1024)
        ars_mult(7, 1024, 2048)
        ars(8, 0, 1024)
        ssquare(8, 0)
        ars(8, 1024, 2048)
        ssquare(8, 1)
        finish(6)
        ars_mult(8, 0, 1024)
        ars_mult(8, 1024, 2048)
        ars(9, 0, 1024)
        ssquare(9, 0)
        ars(9, 1024, 2048)
        ssquare(9, 1)
        finish(7)
        ars_mult(9, 0, 1024)
        ars_mult(9, 1024, 2048)
        ars(10, 0, 1024)
        ssquare(10, 0)
        ars(10, 1024, 2048)
        ssquare(10, 1)
        finish(8)
        ars_mult(10, 0, 1024)
        ars_mult(10, 1024, 2048)
        ars(11, 0, 1024)
        ssquare(11, 0)
        ars(11, 1024, 2048)
        ssquare(11, 1)
        finish(9)
        ars_mult(11, 0, 1024)
        ars_mult(11, 1024, 2048)
        finish(10)
        finish(11)
